import numpy as np
import ml_dtypes


def mxq(x, axis, fmt="e4m3"):
    dtype, down = {"e4m3": (ml_dtypes.float8_e4m3fn, 7), "e5m2": (ml_dtypes.float8_e5m2, 14)}[fmt]
    v = np.moveaxis(np.asarray(x, np.float32).astype(ml_dtypes.bfloat16).astype(np.float64), axis, -1)
    blocks = v.reshape(v.shape[:-1] + (-1, 32))
    amax = np.abs(blocks).max(-1, keepdims=True)
    byte = np.maximum(np.where(amax > 0, np.frexp(amax)[1] - 1 + 127, 0) - down, 1)
    scale = np.exp2(byte - 127.0)
    codes = (blocks / scale).astype(np.float32).astype(dtype).astype(np.float64)
    return np.moveaxis((codes * scale).reshape(v.shape), -1, axis)


WIDE = False


def mx_kscale(k):
    if not WIDE:
        return np.ones(k)
    levels = np.array([10, -10, 5, -5, 0])
    a = np.random.permutation(np.resize(levels, k // 512 * 4)).reshape(k // 512, 4)
    idx = np.arange(k)
    return np.exp2(a[idx // 512, idx % 128 // 32])


BF16 = ml_dtypes.bfloat16


def bf(x):
    return np.asarray(x, np.float32).astype(BF16)


def f64(x):
    return np.asarray(x).astype(np.float64)


E2M1 = np.array([0.0, 0.5, 1.0, 1.5, 2.0, 3.0, 4.0, 6.0, -0.0, -0.5, -1.0, -1.5, -2.0, -3.0, -4.0, -6.0])


def pack_weight(w, fmt):
    k, n = w.shape
    w = f64(bf(w)).reshape(k // 32, 32, n)
    amax = np.abs(w).max(1)
    if fmt == "e4m3":
        byte = np.frexp(amax)[1] - 1 + 127 - 7
    else:
        mant, ex = np.frexp(amax / 6.0)
        byte = np.where(mant > 0.5, ex, ex - 1) + 127
    byte = np.clip(np.where(amax > 0, byte, 1), 1, 254)
    scaled = (w * np.exp2(127.0 - byte)[:, None, :]).reshape(k, n).astype(np.float32)
    by_word = np.ascontiguousarray(scaled.reshape(k // 512, 128, 4, n).transpose(0, 1, 3, 2))
    if fmt == "e4m3":
        words = by_word.astype(ml_dtypes.float8_e4m3fn).view(np.uint8)
    else:
        c = by_word.astype(ml_dtypes.float4_e2m1fn).view(np.uint8) & 0xF
        words = c[..., 0::2] | (c[..., 1::2] << 4)
    return np.ascontiguousarray(words), np.ascontiguousarray(byte.astype(np.uint8).reshape(k // 512, 16, n))


def unpack_weight(words, scales, fmt):
    g, p, n, _ = words.shape
    if fmt == "e4m3":
        vals = np.ascontiguousarray(words).view(ml_dtypes.float8_e4m3fn).astype(np.float64)
    else:
        nib = np.empty((g, p, n, 4), np.uint8)
        nib[..., 0::2] = words & 0xF
        nib[..., 1::2] = words >> 4
        vals = E2M1[nib]
    vals = vals * np.repeat(np.exp2(scales.astype(np.float64) - 127.0), 8, axis=1)[..., None]
    return vals.transpose(0, 1, 3, 2).reshape(g * 512, n)


B, M, F, U = 4096, 4, 512, 256
FMT = "e4m3"


def setup_inputs():
    s = mx_kscale(F)
    limit = np.sqrt(6.0 / (F + U))
    x = bf(np.random.standard_normal((B, M, F)) * s)
    stack = np.random.uniform(-limit, limit, (M, F, U)) / s[None, :, None]
    words, scales = pack_weight(stack.reshape(-1, U), FMT)
    b = bf(np.random.standard_normal((M, U)) * 0.1)
    return {"x": x, "W_words": words, "W_scales": scales, "b": b}


def reference(x, W_words, W_scales, b):
    xq = mxq(f64(x), 2, "e4m3")
    wq = unpack_weight(W_words, W_scales, FMT).reshape(M, F, U)
    y = (xq.transpose(1, 0, 2) @ wq).transpose(1, 0, 2)
    y = np.maximum(y + f64(b)[None, :, :], 0.0)
    return y.reshape(y.shape[0], -1)

@@ -1,0 +1,168 @@
+from contextlib import ExitStack
+
+import concourse.mybir as mybir
+from concourse.masks import make_identity
+
+BF16 = mybir.dt.bfloat16
+F32 = mybir.dt.float32
+I32 = mybir.dt.int32
+U32 = mybir.dt.uint32
+U8 = mybir.dt.uint8
+FP8X4 = mybir.dt.float8_e4m3fn_x4
+
+P = 128
+ROWS = 4096
+MASKS = 4
+K = 512
+U = 256
+BANK = 512
+PAIRS = MASKS // 2
+HALVES = 2
+
+TILES = 2
+CHUNKS = ROWS // (P * TILES)
+LOAD_AHEAD = 7
+SCALAR_RELU = 768
+
+FLOPS = 2 * ROWS * MASKS * K * U
+
+
+def tile_paralleldense_t_e_kernel(tc, x, W_words, W_scales, b, out):
+    nc = tc.nc
+    x_chunks = x.rearrange("(c p t) m k -> c p t (m k)", p=P, t=TILES)
+    out_chunks = out.rearrange("(c p t) n -> c p t n", p=P, t=TILES)
+
+    with ExitStack() as ctx:
+        ctx.enter_context(tc.manual_schedule())
+        keep = ctx.enter_context(tc.tile_pool(name="keep", bufs=1))
+        x_pool = ctx.enter_context(tc.tile_pool(name="x_pool", bufs=LOAD_AHEAD + 1))
+        mx_pool = ctx.enter_context(tc.tile_pool(name="mx_pool", bufs=3))
+        y_pool = ctx.enter_context(tc.tile_pool(name="y_pool", bufs=6))
+        xt_banks = ctx.enter_context(tc.psum_pool(name="xt_banks", bufs=4))
+        acc_banks = ctx.enter_context(tc.psum_pool(name="acc_banks", bufs=4))
+
+        x_tiles = {}
+        grouped_tiles = {}
+        code_tiles = {}
+        plane_tiles = {}
+        y_tiles = {}
+
+        def load_chunk(c):
+            x_sb = x_pool.tile([P, TILES, MASKS * K], BF16, name="x_sb")
+            nc.sync.dma_start(out=x_sb[:], in_=x_chunks[c])
+            x_tiles[c] = x_sb
+
+        def transpose_chunk(c):
+            grouped = mx_pool.tile([P, TILES, MASKS * K], BF16, name="grouped", align_bytes=64)
+            grouped_tiles[c] = grouped
+            for t in range(TILES):
+                x_words = x_tiles[c][:, t, :].bitcast(F32)
+                grouped_words = grouped[:, t, :].bitcast(F32)
+                for pair in range(PAIRS):
+                    xt = xt_banks.tile([P, 2, HALVES, P], F32, name="xt")
+                    for i in range(2):
+                        first = (2 * pair + i) * (K // 2)
+                        for u in range(HALVES):
+                            nc.tensor.transpose(
+                                xt[:, i, u, :],
+                                x_words[:, first + u : first + K // 2 : HALVES],
+                                ident[:],
+                            )
+                    nc.scalar.copy(
+                        out=grouped_words[:, pair * BANK : (pair + 1) * BANK].rearrange(
+                            "p (i r u) -> p i r u", i=2, u=HALVES
+                        ),
+                        in_=xt[:].rearrange("p i u r -> p i r u"),
+                    )
+
+        def quantise_chunk(c):
+            codes = mx_pool.tile([P, TILES, MASKS * P], U32, name="codes", align_bytes=64)
+            planes = mx_pool.tile([P, TILES, MASKS * P], U8, name="planes", align_bytes=64)
+            code_tiles[c] = codes
+            plane_tiles[c] = planes
+            for t in range(TILES):
+                nc.vector.quantize_mx(
+                    out=codes[:, t, :].bitcast(FP8X4),
+                    scales=planes[:, t, :],
+                    in_=grouped_tiles[c][:, t, :],
+                )
+
+        def multiply_chunk(c):
+            y = y_pool.tile([P, TILES, MASKS * U], F32, name="y")
+            y_tiles[c] = y
+            for t in range(TILES):
+                for pair in range(PAIRS):
+                    acc = acc_banks.tile([P, BANK], F32, name="acc")
+                    for i in range(2):
+                        m = 2 * pair + i
+                        rows = slice(m * P, (m + 1) * P)
+                        nc.tensor.matmul_mx(
+                            out=acc[:, i * U : (i + 1) * U],
+                            lhsT=code_tiles[c][:, t, rows].bitcast(FP8X4),
+                            lhsT_scale=plane_tiles[c][:, t, rows],
+                            rhs=w_codes[:, m, :].bitcast(FP8X4),
+                            rhs_scale=w_planes[4 * m : P, :],
+                            start=True,
+                            stop=True,
+                        )
+                    cols = slice(pair * BANK, (pair + 1) * BANK)
+                    nc.vector.tensor_tensor(
+                        out=y[:, t, cols], in0=acc[:], in1=bias[:, cols], op=mybir.AluOpType.add
+                    )
+
+        def finish_chunk(c):
+            y = y_tiles[c]
+            nc.scalar.activation(
+                out=y[:, :, :SCALAR_RELU],
+                in_=y[:, :, :SCALAR_RELU],
+                func=mybir.ActivationFunctionType.Relu,
+            )
+            nc.vector.tensor_scalar_max(y[:, :, SCALAR_RELU:], y[:, :, SCALAR_RELU:], 0.0)
+            nc.sync.dma_start(out=out_chunks[c], in_=y[:])
+
+        ident = keep.tile([P, P], F32, name="ident")
+        make_identity(nc, ident[:])
+
+        w_planes = keep.tile([P, U], U8, name="w_planes", align_bytes=64)
+        nc.vector.memset(w_planes[:].bitcast(I32), 0)
+        w_codes = keep.tile([P, MASKS, U], U32, name="w_codes", align_bytes=64)
+
+        b_row = keep.tile([P, MASKS * U], BF16, name="b_row")
+        nc.vector.memset(b_row[:], 0.0)
+        ones = keep.tile([P, P], BF16, name="ones")
+        nc.vector.memset(ones[:], 1.0)
+        bias = keep.tile([P, MASKS * U], F32, name="bias")
+
+        load_chunk(0)
+        scale_words = W_scales.bitcast(I32)
+        for quadrant in range(4):
+            nc.sync.dma_start(
+                out=w_planes[32 * quadrant : 32 * quadrant + 16, :].bitcast(I32),
+                in_=scale_words[:, 4 * quadrant : 4 * quadrant + 4, :],
+            )
+        nc.sync.dma_start(
+            out=w_codes[:].bitcast(I32),
+            in_=W_words.rearrange("g p n t -> g p (n t)").bitcast(I32).rearrange("g p n -> p g n"),
+        )
+        nc.sync.dma_start(out=b_row[0:1, :], in_=b.rearrange("(o m) u -> o (m u)", o=1))
+        for c in range(1, LOAD_AHEAD):
+            load_chunk(c)
+
+        transpose_chunk(0)
+        for pair in range(PAIRS):
+            cols = slice(pair * BANK, (pair + 1) * BANK)
+            spread = acc_banks.tile([P, BANK], F32, name="acc")
+            nc.tensor.matmul(out=spread[:], lhsT=ones[:], rhs=b_row[:, cols], start=True, stop=True)
+            nc.vector.tensor_copy(out=bias[:, cols], in_=spread[:])
+        quantise_chunk(0)
+        for step in range(1, CHUNKS + 2):
+            if step < CHUNKS:
+                transpose_chunk(step)
+            if step - 1 < CHUNKS:
+                multiply_chunk(step - 1)
+            if step < CHUNKS:
+                quantise_chunk(step)
+            if step >= 2:
+                finish_chunk(step - 2)
+            if step + LOAD_AHEAD - 1 < CHUNKS:
+                load_chunk(step + LOAD_AHEAD - 1)

@@ -22,7 +22,6 @@ HALVES = 2
 TILES = 2
 CHUNKS = ROWS // (P * TILES)
 LOAD_AHEAD = 7
-SCALAR_RELU = 768
 
 FLOPS = 2 * ROWS * MASKS * K * U
 
@@ -90,8 +89,8 @@ def tile_paralleldense_t_e_kernel(tc, x, W_words, W_scales, b, out):
         def multiply_chunk(c):
             y = y_pool.tile([P, TILES, MASKS * U], F32, name="y")
             y_tiles[c] = y
-            for t in range(TILES):
-                for pair in range(PAIRS):
+            for pair in range(PAIRS):
+                for t in range(TILES):
                     acc = acc_banks.tile([P, BANK], F32, name="acc")
                     for i in range(2):
                         m = 2 * pair + i
@@ -109,15 +108,21 @@ def tile_paralleldense_t_e_kernel(tc, x, W_words, W_scales, b, out):
                     nc.vector.tensor_tensor(
                         out=y[:, t, cols], in0=acc[:], in1=bias[:, cols], op=mybir.AluOpType.add
                     )
+                    if pair == 0:
+                        nc.gpsimd.tensor_scalar(
+                            out=y[:, t, cols],
+                            in0=y[:, t, cols],
+                            scalar1=float("inf"),
+                            scalar2=0.0,
+                            op0=mybir.AluOpType.min,
+                            op1=mybir.AluOpType.max,
+                        )
 
         def finish_chunk(c):
             y = y_tiles[c]
             nc.scalar.activation(
-                out=y[:, :, :SCALAR_RELU],
-                in_=y[:, :, :SCALAR_RELU],
-                func=mybir.ActivationFunctionType.Relu,
+                out=y[:, :, BANK:], in_=y[:, :, BANK:], func=mybir.ActivationFunctionType.Relu
             )
-            nc.vector.tensor_scalar_max(y[:, :, SCALAR_RELU:], y[:, :, SCALAR_RELU:], 0.0)
             nc.sync.dma_start(out=out_chunks[c], in_=y[:])
 
         ident = keep.tile([P, P], F32, name="ident")

@@ -22,6 +22,7 @@ HALVES = 2
 TILES = 2
 CHUNKS = ROWS // (P * TILES)
 LOAD_AHEAD = 7
+SCALAR_RELU = 768
 
 FLOPS = 2 * ROWS * MASKS * K * U
 
@@ -46,10 +47,13 @@ def tile_paralleldense_t_e_kernel(tc, x, W_words, W_scales, b, out):
         plane_tiles = {}
         y_tiles = {}
 
-        def load_chunk(c):
-            x_sb = x_pool.tile([P, TILES, MASKS * K], BF16, name="x_sb")
-            nc.sync.dma_start(out=x_sb[:], in_=x_chunks[c])
-            x_tiles[c] = x_sb
+        def load_chunk(c, pieces):
+            x_tiles[c] = x_pool.tile([P, TILES, MASKS * K], BF16, name="x_sb")
+            width = TILES // pieces
+            for t in range(0, TILES, width):
+                nc.sync.dma_start(
+                    out=x_tiles[c][:, t : t + width, :], in_=x_chunks[c][:, t : t + width, :]
+                )
 
         def transpose_chunk(c):
             grouped = mx_pool.tile([P, TILES, MASKS * K], BF16, name="grouped", align_bytes=64)
@@ -89,8 +93,8 @@ def tile_paralleldense_t_e_kernel(tc, x, W_words, W_scales, b, out):
         def multiply_chunk(c):
             y = y_pool.tile([P, TILES, MASKS * U], F32, name="y")
             y_tiles[c] = y
-            for pair in range(PAIRS):
-                for t in range(TILES):
+            for t in range(TILES):
+                for pair in range(PAIRS):
                     acc = acc_banks.tile([P, BANK], F32, name="acc")
                     for i in range(2):
                         m = 2 * pair + i
@@ -108,22 +112,25 @@ def tile_paralleldense_t_e_kernel(tc, x, W_words, W_scales, b, out):
                     nc.vector.tensor_tensor(
                         out=y[:, t, cols], in0=acc[:], in1=bias[:, cols], op=mybir.AluOpType.add
                     )
-                    if pair == 0:
-                        nc.gpsimd.tensor_scalar(
-                            out=y[:, t, cols],
-                            in0=y[:, t, cols],
-                            scalar1=float("inf"),
-                            scalar2=0.0,
-                            op0=mybir.AluOpType.min,
-                            op1=mybir.AluOpType.max,
-                        )
 
-        def finish_chunk(c):
+        def finish_chunk(c, pieces):
             y = y_tiles[c]
-            nc.scalar.activation(
-                out=y[:, :, BANK:], in_=y[:, :, BANK:], func=mybir.ActivationFunctionType.Relu
-            )
-            nc.sync.dma_start(out=out_chunks[c], in_=y[:])
+            width = TILES // pieces
+            for t in range(0, TILES, width):
+                nc.scalar.activation(
+                    out=y[:, t : t + width, :SCALAR_RELU],
+                    in_=y[:, t : t + width, :SCALAR_RELU],
+                    func=mybir.ActivationFunctionType.Relu,
+                )
+                nc.gpsimd.tensor_scalar(
+                    out=y[:, t : t + width, SCALAR_RELU:],
+                    in0=y[:, t : t + width, SCALAR_RELU:],
+                    scalar1=float("inf"),
+                    scalar2=0.0,
+                    op0=mybir.AluOpType.min,
+                    op1=mybir.AluOpType.max,
+                )
+                nc.sync.dma_start(out=out_chunks[c][:, t : t + width, :], in_=y[:, t : t + width, :])
 
         ident = keep.tile([P, P], F32, name="ident")
         make_identity(nc, ident[:])
@@ -138,7 +145,8 @@ def tile_paralleldense_t_e_kernel(tc, x, W_words, W_scales, b, out):
         nc.vector.memset(ones[:], 1.0)
         bias = keep.tile([P, MASKS * U], F32, name="bias")
 
-        load_chunk(0)
+        load_chunk(0, TILES)
+        load_chunk(1, 1)
         scale_words = W_scales.bitcast(I32)
         for quadrant in range(4):
             nc.sync.dma_start(
@@ -150,16 +158,16 @@ def tile_paralleldense_t_e_kernel(tc, x, W_words, W_scales, b, out):
             in_=W_words.rearrange("g p n t -> g p (n t)").bitcast(I32).rearrange("g p n -> p g n"),
         )
         nc.sync.dma_start(out=b_row[0:1, :], in_=b.rearrange("(o m) u -> o (m u)", o=1))
-        for c in range(1, LOAD_AHEAD):
-            load_chunk(c)
+        for c in range(2, LOAD_AHEAD):
+            load_chunk(c, 1)
 
         transpose_chunk(0)
+        quantise_chunk(0)
         for pair in range(PAIRS):
             cols = slice(pair * BANK, (pair + 1) * BANK)
             spread = acc_banks.tile([P, BANK], F32, name="acc")
             nc.tensor.matmul(out=spread[:], lhsT=ones[:], rhs=b_row[:, cols], start=True, stop=True)
             nc.vector.tensor_copy(out=bias[:, cols], in_=spread[:])
-        quantise_chunk(0)
         for step in range(1, CHUNKS + 2):
             if step < CHUNKS:
                 transpose_chunk(step)
@@ -168,6 +176,6 @@ def tile_paralleldense_t_e_kernel(tc, x, W_words, W_scales, b, out):
             if step < CHUNKS:
                 quantise_chunk(step)
             if step >= 2:
-                finish_chunk(step - 2)
+                finish_chunk(step - 2, TILES if step - 2 == CHUNKS - 1 else 1)
             if step + LOAD_AHEAD - 1 < CHUNKS:
-                load_chunk(step + LOAD_AHEAD - 1)
+                load_chunk(step + LOAD_AHEAD - 1, 1)

@@ -21,7 +21,9 @@ HALVES = 2
 
 TILES = 2
 CHUNKS = ROWS // (P * TILES)
-LOAD_AHEAD = 7
+ROW_TILES = CHUNKS * TILES
+X_BUFS = 8
+AHEAD = 2
 SCALAR_RELU = 768
 
 FLOPS = 2 * ROWS * MASKS * K * U
@@ -35,8 +37,8 @@ def tile_paralleldense_t_e_kernel(tc, x, W_words, W_scales, b, out):
     with ExitStack() as ctx:
         ctx.enter_context(tc.manual_schedule())
         keep = ctx.enter_context(tc.tile_pool(name="keep", bufs=1))
-        x_pool = ctx.enter_context(tc.tile_pool(name="x_pool", bufs=LOAD_AHEAD + 1))
-        mx_pool = ctx.enter_context(tc.tile_pool(name="mx_pool", bufs=3))
+        x_pool = ctx.enter_context(tc.tile_pool(name="x_pool", bufs=X_BUFS))
+        mx_pool = ctx.enter_context(tc.tile_pool(name="mx_pool", bufs=4))
         y_pool = ctx.enter_context(tc.tile_pool(name="y_pool", bufs=6))
         xt_banks = ctx.enter_context(tc.psum_pool(name="xt_banks", bufs=4))
         acc_banks = ctx.enter_context(tc.psum_pool(name="acc_banks", bufs=4))
@@ -55,82 +57,81 @@ def tile_paralleldense_t_e_kernel(tc, x, W_words, W_scales, b, out):
                     out=x_tiles[c][:, t : t + width, :], in_=x_chunks[c][:, t : t + width, :]
                 )
 
-        def transpose_chunk(c):
-            grouped = mx_pool.tile([P, TILES, MASKS * K], BF16, name="grouped", align_bytes=64)
-            grouped_tiles[c] = grouped
-            for t in range(TILES):
-                x_words = x_tiles[c][:, t, :].bitcast(F32)
-                grouped_words = grouped[:, t, :].bitcast(F32)
-                for pair in range(PAIRS):
-                    xt = xt_banks.tile([P, 2, HALVES, P], F32, name="xt")
-                    for i in range(2):
-                        first = (2 * pair + i) * (K // 2)
-                        for u in range(HALVES):
-                            nc.tensor.transpose(
-                                xt[:, i, u, :],
-                                x_words[:, first + u : first + K // 2 : HALVES],
-                                ident[:],
-                            )
-                    nc.scalar.copy(
-                        out=grouped_words[:, pair * BANK : (pair + 1) * BANK].rearrange(
-                            "p (i r u) -> p i r u", i=2, u=HALVES
-                        ),
-                        in_=xt[:].rearrange("p i u r -> p i r u"),
-                    )
-
-        def quantise_chunk(c):
-            codes = mx_pool.tile([P, TILES, MASKS * P], U32, name="codes", align_bytes=64)
-            planes = mx_pool.tile([P, TILES, MASKS * P], U8, name="planes", align_bytes=64)
-            code_tiles[c] = codes
-            plane_tiles[c] = planes
-            for t in range(TILES):
-                nc.vector.quantize_mx(
-                    out=codes[:, t, :].bitcast(FP8X4),
-                    scales=planes[:, t, :],
-                    in_=grouped_tiles[c][:, t, :],
-                )
-
-        def multiply_chunk(c):
-            y = y_pool.tile([P, TILES, MASKS * U], F32, name="y")
-            y_tiles[c] = y
-            for t in range(TILES):
-                for pair in range(PAIRS):
-                    acc = acc_banks.tile([P, BANK], F32, name="acc")
-                    for i in range(2):
-                        m = 2 * pair + i
-                        rows = slice(m * P, (m + 1) * P)
-                        nc.tensor.matmul_mx(
-                            out=acc[:, i * U : (i + 1) * U],
-                            lhsT=code_tiles[c][:, t, rows].bitcast(FP8X4),
-                            lhsT_scale=plane_tiles[c][:, t, rows],
-                            rhs=w_codes[:, m, :].bitcast(FP8X4),
-                            rhs_scale=w_planes[4 * m : P, :],
-                            start=True,
-                            stop=True,
+        def transpose_tile(i):
+            grouped = mx_pool.tile([P, MASKS * K], BF16, name="grouped", align_bytes=64)
+            grouped_tiles[i] = grouped
+            x_words = x_tiles[i // TILES][:, i % TILES, :].bitcast(F32)
+            grouped_words = grouped[:].bitcast(F32)
+            for pair in range(PAIRS):
+                xt = xt_banks.tile([P, 2, HALVES, P], F32, name="xt")
+                for j in range(2):
+                    first = (2 * pair + j) * (K // 2)
+                    for u in range(HALVES):
+                        nc.tensor.transpose(
+                            xt[:, j, u, :],
+                            x_words[:, first + u : first + K // 2 : HALVES],
+                            ident[:],
                         )
-                    cols = slice(pair * BANK, (pair + 1) * BANK)
-                    nc.vector.tensor_tensor(
-                        out=y[:, t, cols], in0=acc[:], in1=bias[:, cols], op=mybir.AluOpType.add
-                    )
+                nc.scalar.copy(
+                    out=grouped_words[:, pair * BANK : (pair + 1) * BANK].rearrange(
+                        "p (j r u) -> p j r u", j=2, u=HALVES
+                    ),
+                    in_=xt[:].rearrange("p j u r -> p j r u"),
+                )
 
-        def finish_chunk(c, pieces):
-            y = y_tiles[c]
-            width = TILES // pieces
-            for t in range(0, TILES, width):
-                nc.scalar.activation(
-                    out=y[:, t : t + width, :SCALAR_RELU],
-                    in_=y[:, t : t + width, :SCALAR_RELU],
-                    func=mybir.ActivationFunctionType.Relu,
+        def quantise_tile(i):
+            codes = mx_pool.tile([P, MASKS * P], U32, name="codes", align_bytes=64)
+            planes = mx_pool.tile([P, MASKS * P], U8, name="planes", align_bytes=64)
+            code_tiles[i] = codes
+            plane_tiles[i] = planes
+            nc.vector.quantize_mx(
+                out=codes[:].bitcast(FP8X4), scales=planes[:], in_=grouped_tiles[i][:]
+            )
+
+        def multiply_tile(i):
+            if i % TILES == 0:
+                y_tiles[i // TILES] = y_pool.tile([P, TILES, MASKS * U], F32, name="y")
+            y = y_tiles[i // TILES]
+            for pair in range(PAIRS):
+                acc = acc_banks.tile([P, BANK], F32, name="acc")
+                for j in range(2):
+                    m = 2 * pair + j
+                    rows = slice(m * P, (m + 1) * P)
+                    nc.tensor.matmul_mx(
+                        out=acc[:, j * U : (j + 1) * U],
+                        lhsT=code_tiles[i][:, rows].bitcast(FP8X4),
+                        lhsT_scale=plane_tiles[i][:, rows],
+                        rhs=w_codes[:, m, :].bitcast(FP8X4),
+                        rhs_scale=w_planes[4 * m : P, :],
+                        start=True,
+                        stop=True,
+                    )
+                cols = slice(pair * BANK, (pair + 1) * BANK)
+                nc.vector.tensor_tensor(
+                    out=y[:, i % TILES, cols], in0=acc[:], in1=bias[:, cols], op=mybir.AluOpType.add
                 )
-                nc.gpsimd.tensor_scalar(
-                    out=y[:, t : t + width, SCALAR_RELU:],
-                    in0=y[:, t : t + width, SCALAR_RELU:],
-                    scalar1=float("inf"),
-                    scalar2=0.0,
-                    op0=mybir.AluOpType.min,
-                    op1=mybir.AluOpType.max,
-                )
-                nc.sync.dma_start(out=out_chunks[c][:, t : t + width, :], in_=y[:, t : t + width, :])
+
+        def relu_tile(i):
+            y_row = y_tiles[i // TILES][:, i % TILES, :]
+            nc.scalar.activation(
+                out=y_row[:, :SCALAR_RELU],
+                in_=y_row[:, :SCALAR_RELU],
+                func=mybir.ActivationFunctionType.Relu,
+            )
+            nc.gpsimd.tensor_scalar(
+                out=y_row[:, SCALAR_RELU:],
+                in0=y_row[:, SCALAR_RELU:],
+                scalar1=float("inf"),
+                scalar2=0.0,
+                op0=mybir.AluOpType.min,
+                op1=mybir.AluOpType.max,
+            )
+
+        def store_tiles(c, first, count):
+            nc.sync.dma_start(
+                out=out_chunks[c][:, first : first + count, :],
+                in_=y_tiles[c][:, first : first + count, :],
+            )
 
         ident = keep.tile([P, P], F32, name="ident")
         make_identity(nc, ident[:])
@@ -158,24 +159,32 @@ def tile_paralleldense_t_e_kernel(tc, x, W_words, W_scales, b, out):
             in_=W_words.rearrange("g p n t -> g p (n t)").bitcast(I32).rearrange("g p n -> p g n"),
         )
         nc.sync.dma_start(out=b_row[0:1, :], in_=b.rearrange("(o m) u -> o (m u)", o=1))
-        for c in range(2, LOAD_AHEAD):
+        for c in range(2, X_BUFS):
             load_chunk(c, 1)
 
-        transpose_chunk(0)
-        quantise_chunk(0)
+        for i in range(AHEAD):
+            transpose_tile(i)
+        quantise_tile(0)
         for pair in range(PAIRS):
             cols = slice(pair * BANK, (pair + 1) * BANK)
             spread = acc_banks.tile([P, BANK], F32, name="acc")
             nc.tensor.matmul(out=spread[:], lhsT=ones[:], rhs=b_row[:, cols], start=True, stop=True)
             nc.vector.tensor_copy(out=bias[:, cols], in_=spread[:])
-        for step in range(1, CHUNKS + 2):
-            if step < CHUNKS:
-                transpose_chunk(step)
-            if step - 1 < CHUNKS:
-                multiply_chunk(step - 1)
-            if step < CHUNKS:
-                quantise_chunk(step)
-            if step >= 2:
-                finish_chunk(step - 2, TILES if step - 2 == CHUNKS - 1 else 1)
-            if step + LOAD_AHEAD - 1 < CHUNKS:
-                load_chunk(step + LOAD_AHEAD - 1, 1)
+        quantise_tile(1)
+        for i in range(ROW_TILES + 1):
+            if i + AHEAD < ROW_TILES:
+                transpose_tile(i + AHEAD)
+            if i < ROW_TILES:
+                multiply_tile(i)
+            if i + AHEAD < ROW_TILES:
+                quantise_tile(i + AHEAD)
+            if i >= 1:
+                done = i - 1
+                c = done // TILES
+                relu_tile(done)
+                if c == CHUNKS - 1:
+                    store_tiles(c, done % TILES, 1)
+                elif done % TILES == TILES - 1:
+                    store_tiles(c, 0, TILES)
+                    if c + X_BUFS < CHUNKS:
+                        load_chunk(c + X_BUFS, 1)

@@ -24,7 +24,7 @@ CHUNKS = ROWS // (P * TILES)
 ROW_TILES = CHUNKS * TILES
 X_BUFS = 8
 AHEAD = 2
-SCALAR_RELU = 768
+SCALAR_RELU = 640
 
 FLOPS = 2 * ROWS * MASKS * K * U
 

@@ -23,7 +23,7 @@ TILES = 2
 CHUNKS = ROWS // (P * TILES)
 ROW_TILES = CHUNKS * TILES
 X_BUFS = 8
-AHEAD = 2
+AHEAD = 3
 SCALAR_RELU = 640
 
 FLOPS = 2 * ROWS * MASKS * K * U
@@ -49,13 +49,13 @@ def tile_paralleldense_t_e_kernel(tc, x, W_words, W_scales, b, out):
         plane_tiles = {}
         y_tiles = {}
 
-        def load_chunk(c, pieces):
-            x_tiles[c] = x_pool.tile([P, TILES, MASKS * K], BF16, name="x_sb")
-            width = TILES // pieces
-            for t in range(0, TILES, width):
-                nc.sync.dma_start(
-                    out=x_tiles[c][:, t : t + width, :], in_=x_chunks[c][:, t : t + width, :]
-                )
+        def load_tiles(c, first, count):
+            if first == 0:
+                x_tiles[c] = x_pool.tile([P, TILES, MASKS * K], BF16, name="x_sb")
+            nc.sync.dma_start(
+                out=x_tiles[c][:, first : first + count, :],
+                in_=x_chunks[c][:, first : first + count, :],
+            )
 
         def transpose_tile(i):
             grouped = mx_pool.tile([P, MASKS * K], BF16, name="grouped", align_bytes=64)
@@ -146,8 +146,8 @@ def tile_paralleldense_t_e_kernel(tc, x, W_words, W_scales, b, out):
         nc.vector.memset(ones[:], 1.0)
         bias = keep.tile([P, MASKS * U], F32, name="bias")
 
-        load_chunk(0, TILES)
-        load_chunk(1, 1)
+        for i in range(AHEAD):
+            load_tiles(i // TILES, i % TILES, 1)
         scale_words = W_scales.bitcast(I32)
         for quadrant in range(4):
             nc.sync.dma_start(
@@ -159,25 +159,25 @@ def tile_paralleldense_t_e_kernel(tc, x, W_words, W_scales, b, out):
             in_=W_words.rearrange("g p n t -> g p (n t)").bitcast(I32).rearrange("g p n -> p g n"),
         )
         nc.sync.dma_start(out=b_row[0:1, :], in_=b.rearrange("(o m) u -> o (m u)", o=1))
+        for i in range(AHEAD, 2 * TILES):
+            load_tiles(i // TILES, i % TILES, 1)
         for c in range(2, X_BUFS):
-            load_chunk(c, 1)
+            load_tiles(c, 0, TILES)
 
         for i in range(AHEAD):
             transpose_tile(i)
-        quantise_tile(0)
+        for i in range(AHEAD - 1):
+            quantise_tile(i)
         for pair in range(PAIRS):
             cols = slice(pair * BANK, (pair + 1) * BANK)
             spread = acc_banks.tile([P, BANK], F32, name="acc")
             nc.tensor.matmul(out=spread[:], lhsT=ones[:], rhs=b_row[:, cols], start=True, stop=True)
             nc.vector.tensor_copy(out=bias[:, cols], in_=spread[:])
-        quantise_tile(1)
         for i in range(ROW_TILES + 1):
-            if i + AHEAD < ROW_TILES:
-                transpose_tile(i + AHEAD)
             if i < ROW_TILES:
                 multiply_tile(i)
-            if i + AHEAD < ROW_TILES:
-                quantise_tile(i + AHEAD)
+            if i + AHEAD - 1 < ROW_TILES:
+                quantise_tile(i + AHEAD - 1)
             if i >= 1:
                 done = i - 1
                 c = done // TILES
@@ -187,4 +187,6 @@ def tile_paralleldense_t_e_kernel(tc, x, W_words, W_scales, b, out):
                 elif done % TILES == TILES - 1:
                     store_tiles(c, 0, TILES)
                     if c + X_BUFS < CHUNKS:
-                        load_chunk(c + X_BUFS, 1)
+                        load_tiles(c + X_BUFS, 0, TILES)
+            if i + AHEAD < ROW_TILES:
+                transpose_tile(i + AHEAD)

@@ -19,10 +19,11 @@ BANK = 512
 PAIRS = MASKS // 2
 HALVES = 2
 
-TILES = 2
+TILES = 4
 CHUNKS = ROWS // (P * TILES)
 ROW_TILES = CHUNKS * TILES
-X_BUFS = 8
+STORE = 2
+FRESH = 4
 AHEAD = 3
 SCALAR_RELU = 640
 
@@ -37,9 +38,8 @@ def tile_paralleldense_t_e_kernel(tc, x, W_words, W_scales, b, out):
     with ExitStack() as ctx:
         ctx.enter_context(tc.manual_schedule())
         keep = ctx.enter_context(tc.tile_pool(name="keep", bufs=1))
-        x_pool = ctx.enter_context(tc.tile_pool(name="x_pool", bufs=X_BUFS))
+        xy_pool = ctx.enter_context(tc.tile_pool(name="xy_pool", bufs=CHUNKS + FRESH))
         mx_pool = ctx.enter_context(tc.tile_pool(name="mx_pool", bufs=4))
-        y_pool = ctx.enter_context(tc.tile_pool(name="y_pool", bufs=6))
         xt_banks = ctx.enter_context(tc.psum_pool(name="xt_banks", bufs=4))
         acc_banks = ctx.enter_context(tc.psum_pool(name="acc_banks", bufs=4))
 
@@ -51,7 +51,7 @@ def tile_paralleldense_t_e_kernel(tc, x, W_words, W_scales, b, out):
 
         def load_tiles(c, first, count):
             if first == 0:
-                x_tiles[c] = x_pool.tile([P, TILES, MASKS * K], BF16, name="x_sb")
+                x_tiles[c] = xy_pool.tile([P, TILES, MASKS * K], BF16, name="xy")
             nc.sync.dma_start(
                 out=x_tiles[c][:, first : first + count, :],
                 in_=x_chunks[c][:, first : first + count, :],
@@ -90,7 +90,7 @@ def tile_paralleldense_t_e_kernel(tc, x, W_words, W_scales, b, out):
 
         def multiply_tile(i):
             if i % TILES == 0:
-                y_tiles[i // TILES] = y_pool.tile([P, TILES, MASKS * U], F32, name="y")
+                y_tiles[i // TILES] = xy_pool.tile([P, TILES, MASKS * U], F32, name="xy")
             y = y_tiles[i // TILES]
             for pair in range(PAIRS):
                 acc = acc_banks.tile([P, BANK], F32, name="acc")
@@ -127,10 +127,11 @@ def tile_paralleldense_t_e_kernel(tc, x, W_words, W_scales, b, out):
                 op1=mybir.AluOpType.max,
             )
 
-        def store_tiles(c, first, count):
+        def store_tiles(first, count):
+            t = first % TILES
             nc.sync.dma_start(
-                out=out_chunks[c][:, first : first + count, :],
-                in_=y_tiles[c][:, first : first + count, :],
+                out=out_chunks[first // TILES][:, t : t + count, :],
+                in_=y_tiles[first // TILES][:, t : t + count, :],
             )
 
         ident = keep.tile([P, P], F32, name="ident")
@@ -159,9 +160,11 @@ def tile_paralleldense_t_e_kernel(tc, x, W_words, W_scales, b, out):
             in_=W_words.rearrange("g p n t -> g p (n t)").bitcast(I32).rearrange("g p n -> p g n"),
         )
         nc.sync.dma_start(out=b_row[0:1, :], in_=b.rearrange("(o m) u -> o (m u)", o=1))
-        for i in range(AHEAD, 2 * TILES):
+        for i in range(AHEAD, TILES):
             load_tiles(i // TILES, i % TILES, 1)
-        for c in range(2, X_BUFS):
+        load_tiles(1, 0, TILES // 2)
+        load_tiles(1, TILES // 2, TILES // 2)
+        for c in range(2, CHUNKS):
             load_tiles(c, 0, TILES)
 
         for i in range(AHEAD):
@@ -180,13 +183,10 @@ def tile_paralleldense_t_e_kernel(tc, x, W_words, W_scales, b, out):
                 quantise_tile(i + AHEAD - 1)
             if i >= 1:
                 done = i - 1
-                c = done // TILES
                 relu_tile(done)
-                if c == CHUNKS - 1:
-                    store_tiles(c, done % TILES, 1)
-                elif done % TILES == TILES - 1:
-                    store_tiles(c, 0, TILES)
-                    if c + X_BUFS < CHUNKS:
-                        load_tiles(c + X_BUFS, 0, TILES)
+                if done >= ROW_TILES - STORE:
+                    store_tiles(done, 1)
+                elif done % STORE == STORE - 1:
+                    store_tiles(done - STORE + 1, STORE)
             if i + AHEAD < ROW_TILES:
                 transpose_tile(i + AHEAD)

@@ -19,11 +19,12 @@ BANK = 512
 PAIRS = MASKS // 2
 HALVES = 2
 
-TILES = 4
+TILES = 8
 CHUNKS = ROWS // (P * TILES)
 ROW_TILES = CHUNKS * TILES
-STORE = 2
-FRESH = 4
+FRESH = 2
+LOADS = (1, 1, 1, 1, 2, 2, 4, 4, 8, 8)
+STORES = (8, 8, 4, 4, 2, 2, 1, 1, 1, 1)
 AHEAD = 3
 SCALAR_RELU = 640
 
@@ -49,13 +50,12 @@ def tile_paralleldense_t_e_kernel(tc, x, W_words, W_scales, b, out):
         plane_tiles = {}
         y_tiles = {}
 
-        def load_tiles(c, first, count):
-            if first == 0:
+        def load_tiles(first, count):
+            c = first // TILES
+            t = first % TILES
+            if t == 0:
                 x_tiles[c] = xy_pool.tile([P, TILES, MASKS * K], BF16, name="xy")
-            nc.sync.dma_start(
-                out=x_tiles[c][:, first : first + count, :],
-                in_=x_chunks[c][:, first : first + count, :],
-            )
+            nc.sync.dma_start(out=x_tiles[c][:, t : t + count, :], in_=x_chunks[c][:, t : t + count, :])
 
         def transpose_tile(i):
             grouped = mx_pool.tile([P, MASKS * K], BF16, name="grouped", align_bytes=64)
@@ -147,25 +147,25 @@ def tile_paralleldense_t_e_kernel(tc, x, W_words, W_scales, b, out):
         nc.vector.memset(ones[:], 1.0)
         bias = keep.tile([P, MASKS * U], F32, name="bias")
 
-        for i in range(AHEAD):
-            load_tiles(i // TILES, i % TILES, 1)
-        scale_words = W_scales.bitcast(I32)
-        for quadrant in range(4):
+        def load_weights():
+            scale_words = W_scales.bitcast(I32)
+            for quadrant in range(4):
+                nc.sync.dma_start(
+                    out=w_planes[32 * quadrant : 32 * quadrant + 16, :].bitcast(I32),
+                    in_=scale_words[:, 4 * quadrant : 4 * quadrant + 4, :],
+                )
             nc.sync.dma_start(
-                out=w_planes[32 * quadrant : 32 * quadrant + 16, :].bitcast(I32),
-                in_=scale_words[:, 4 * quadrant : 4 * quadrant + 4, :],
+                out=w_codes[:].bitcast(I32),
+                in_=W_words.rearrange("g p n t -> g p (n t)").bitcast(I32).rearrange("g p n -> p g n"),
             )
-        nc.sync.dma_start(
-            out=w_codes[:].bitcast(I32),
-            in_=W_words.rearrange("g p n t -> g p (n t)").bitcast(I32).rearrange("g p n -> p g n"),
-        )
-        nc.sync.dma_start(out=b_row[0:1, :], in_=b.rearrange("(o m) u -> o (m u)", o=1))
-        for i in range(AHEAD, TILES):
-            load_tiles(i // TILES, i % TILES, 1)
-        load_tiles(1, 0, TILES // 2)
-        load_tiles(1, TILES // 2, TILES // 2)
-        for c in range(2, CHUNKS):
-            load_tiles(c, 0, TILES)
+            nc.sync.dma_start(out=b_row[0:1, :], in_=b.rearrange("(o m) u -> o (m u)", o=1))
+
+        loaded = 0
+        for count in LOADS:
+            if loaded == AHEAD:
+                load_weights()
+            load_tiles(loaded, count)
+            loaded += count
 
         for i in range(AHEAD):
             transpose_tile(i)
@@ -176,17 +176,18 @@ def tile_paralleldense_t_e_kernel(tc, x, W_words, W_scales, b, out):
             spread = acc_banks.tile([P, BANK], F32, name="acc")
             nc.tensor.matmul(out=spread[:], lhsT=ones[:], rhs=b_row[:, cols], start=True, stop=True)
             nc.vector.tensor_copy(out=bias[:, cols], in_=spread[:])
+        stores_done = 0
+        stored = 0
         for i in range(ROW_TILES + 1):
             if i < ROW_TILES:
                 multiply_tile(i)
             if i + AHEAD - 1 < ROW_TILES:
                 quantise_tile(i + AHEAD - 1)
             if i >= 1:
-                done = i - 1
-                relu_tile(done)
-                if done >= ROW_TILES - STORE:
-                    store_tiles(done, 1)
-                elif done % STORE == STORE - 1:
-                    store_tiles(done - STORE + 1, STORE)
+                relu_tile(i - 1)
+                if i == stored + STORES[stores_done]:
+                    store_tiles(stored, STORES[stores_done])
+                    stored = i
+                    stores_done += 1
             if i + AHEAD < ROW_TILES:
                 transpose_tile(i + AHEAD)

@@ -24,7 +24,8 @@ CHUNKS = ROWS // (P * TILES)
 ROW_TILES = CHUNKS * TILES
 FRESH = 2
 LOADS = (1, 1, 1, 1, 2, 2, 4, 4, 8, 8)
-STORES = (8, 8, 4, 4, 2, 2, 1, 1, 1, 1)
+STORES = (8, 8, 4, 4, 2, 2, 1, 1, 1)
+WARM_UP = 5
 AHEAD = 3
 SCALAR_RELU = 640
 
@@ -111,16 +112,17 @@ def tile_paralleldense_t_e_kernel(tc, x, W_words, W_scales, b, out):
                     out=y[:, i % TILES, cols], in0=acc[:], in1=bias[:, cols], op=mybir.AluOpType.add
                 )
 
-        def relu_tile(i):
+        def relu_columns(i, first, count, scalar_share):
             y_row = y_tiles[i // TILES][:, i % TILES, :]
+            split = first + scalar_share
             nc.scalar.activation(
-                out=y_row[:, :SCALAR_RELU],
-                in_=y_row[:, :SCALAR_RELU],
+                out=y_row[:, first:split],
+                in_=y_row[:, first:split],
                 func=mybir.ActivationFunctionType.Relu,
             )
             nc.gpsimd.tensor_scalar(
-                out=y_row[:, SCALAR_RELU:],
-                in0=y_row[:, SCALAR_RELU:],
+                out=y_row[:, split : first + count],
+                in0=y_row[:, split : first + count],
                 scalar1=float("inf"),
                 scalar2=0.0,
                 op0=mybir.AluOpType.min,
@@ -134,6 +136,12 @@ def tile_paralleldense_t_e_kernel(tc, x, W_words, W_scales, b, out):
                 in_=y_tiles[first // TILES][:, t : t + count, :],
             )
 
+        ones = keep.tile([P, BANK], BF16, name="ones")
+        nc.vector.memset(ones[:], 1.0)
+        unread = acc_banks.tile([P, BANK], F32, name="acc")
+        for n in range(WARM_UP):
+            nc.tensor.matmul(out=unread[:], lhsT=ones[:, :P], rhs=ones[:], start=True, stop=True)
+
         ident = keep.tile([P, P], F32, name="ident")
         make_identity(nc, ident[:])
 
@@ -143,8 +151,6 @@ def tile_paralleldense_t_e_kernel(tc, x, W_words, W_scales, b, out):
 
         b_row = keep.tile([P, MASKS * U], BF16, name="b_row")
         nc.vector.memset(b_row[:], 0.0)
-        ones = keep.tile([P, P], BF16, name="ones")
-        nc.vector.memset(ones[:], 1.0)
         bias = keep.tile([P, MASKS * U], F32, name="bias")
 
         def load_weights():
@@ -174,20 +180,28 @@ def tile_paralleldense_t_e_kernel(tc, x, W_words, W_scales, b, out):
         for pair in range(PAIRS):
             cols = slice(pair * BANK, (pair + 1) * BANK)
             spread = acc_banks.tile([P, BANK], F32, name="acc")
-            nc.tensor.matmul(out=spread[:], lhsT=ones[:], rhs=b_row[:, cols], start=True, stop=True)
+            nc.tensor.matmul(out=spread[:], lhsT=ones[:, :P], rhs=b_row[:, cols], start=True, stop=True)
             nc.vector.tensor_copy(out=bias[:, cols], in_=spread[:])
         stores_done = 0
         stored = 0
-        for i in range(ROW_TILES + 1):
-            if i < ROW_TILES:
-                multiply_tile(i)
+        for i in range(ROW_TILES):
+            multiply_tile(i)
             if i + AHEAD - 1 < ROW_TILES:
                 quantise_tile(i + AHEAD - 1)
             if i >= 1:
-                relu_tile(i - 1)
+                relu_columns(i - 1, 0, MASKS * U, SCALAR_RELU)
                 if i == stored + STORES[stores_done]:
                     store_tiles(stored, STORES[stores_done])
                     stored = i
                     stores_done += 1
             if i + AHEAD < ROW_TILES:
                 transpose_tile(i + AHEAD)
+
+        last = ROW_TILES - 1
+        for pair in range(PAIRS):
+            cols = slice(pair * BANK, (pair + 1) * BANK)
+            relu_columns(last, pair * BANK, BANK, SCALAR_RELU // PAIRS)
+            nc.sync.dma_start(
+                out=out_chunks[last // TILES][:, last % TILES, cols],
+                in_=y_tiles[last // TILES][:, last % TILES, cols],
+            )

@@ -25,7 +25,6 @@ ROW_TILES = CHUNKS * TILES
 FRESH = 2
 LOADS = (1, 1, 1, 1, 2, 2, 4, 4, 8, 8)
 STORES = (8, 8, 4, 4, 2, 2, 1, 1, 1)
-WARM_UP = 5
 AHEAD = 3
 SCALAR_RELU = 640
 
@@ -136,12 +135,6 @@ def tile_paralleldense_t_e_kernel(tc, x, W_words, W_scales, b, out):
                 in_=y_tiles[first // TILES][:, t : t + count, :],
             )
 
-        ones = keep.tile([P, BANK], BF16, name="ones")
-        nc.vector.memset(ones[:], 1.0)
-        unread = acc_banks.tile([P, BANK], F32, name="acc")
-        for n in range(WARM_UP):
-            nc.tensor.matmul(out=unread[:], lhsT=ones[:, :P], rhs=ones[:], start=True, stop=True)
-
         ident = keep.tile([P, P], F32, name="ident")
         make_identity(nc, ident[:])
 
@@ -151,25 +144,28 @@ def tile_paralleldense_t_e_kernel(tc, x, W_words, W_scales, b, out):
 
         b_row = keep.tile([P, MASKS * U], BF16, name="b_row")
         nc.vector.memset(b_row[:], 0.0)
+        ones = keep.tile([P, P], BF16, name="ones")
+        nc.vector.memset(ones[:], 1.0)
         bias = keep.tile([P, MASKS * U], F32, name="bias")
 
-        def load_weights():
+        def load_scales_and_bias():
             scale_words = W_scales.bitcast(I32)
             for quadrant in range(4):
                 nc.sync.dma_start(
                     out=w_planes[32 * quadrant : 32 * quadrant + 16, :].bitcast(I32),
                     in_=scale_words[:, 4 * quadrant : 4 * quadrant + 4, :],
                 )
-            nc.sync.dma_start(
-                out=w_codes[:].bitcast(I32),
-                in_=W_words.rearrange("g p n t -> g p (n t)").bitcast(I32).rearrange("g p n -> p g n"),
-            )
             nc.sync.dma_start(out=b_row[0:1, :], in_=b.rearrange("(o m) u -> o (m u)", o=1))
 
         loaded = 0
         for count in LOADS:
+            if loaded == AHEAD - 1:
+                load_scales_and_bias()
             if loaded == AHEAD:
-                load_weights()
+                nc.sync.dma_start(
+                    out=w_codes[:].bitcast(I32),
+                    in_=W_words.rearrange("g p n t -> g p (n t)").bitcast(I32).rearrange("g p n -> p g n"),
+                )
             load_tiles(loaded, count)
             loaded += count
 
@@ -180,8 +176,11 @@ def tile_paralleldense_t_e_kernel(tc, x, W_words, W_scales, b, out):
         for pair in range(PAIRS):
             cols = slice(pair * BANK, (pair + 1) * BANK)
             spread = acc_banks.tile([P, BANK], F32, name="acc")
-            nc.tensor.matmul(out=spread[:], lhsT=ones[:, :P], rhs=b_row[:, cols], start=True, stop=True)
-            nc.vector.tensor_copy(out=bias[:, cols], in_=spread[:])
+            nc.tensor.matmul(out=spread[:], lhsT=ones[:], rhs=b_row[:, cols], start=True, stop=True)
+            if pair == 0:
+                nc.vector.tensor_copy(out=bias[:, cols], in_=spread[:])
+            else:
+                nc.scalar.copy(out=bias[:, cols], in_=spread[:])
         stores_done = 0
         stored = 0
         for i in range(ROW_TILES):

from contextlib import ExitStack

import concourse.mybir as mybir
from concourse.masks import make_identity

BF16 = mybir.dt.bfloat16
F32 = mybir.dt.float32
I32 = mybir.dt.int32
U32 = mybir.dt.uint32
U8 = mybir.dt.uint8
FP8X4 = mybir.dt.float8_e4m3fn_x4

P = 128
ROWS = 4096
MASKS = 4
K = 512
U = 256
BANK = 512
PAIRS = MASKS // 2
HALVES = 2

TILES = 8
CHUNKS = ROWS // (P * TILES)
ROW_TILES = CHUNKS * TILES
FRESH = 2
LOADS = (1, 1, 1, 1, 2, 2, 4, 4, 8, 8)
STORES = (8, 8, 4, 4, 2, 2, 1, 1, 1)
AHEAD = 3
SCALAR_RELU = 640

FLOPS = 2 * ROWS * MASKS * K * U


def tile_paralleldense_t_e_kernel(tc, x, W_words, W_scales, b, out):
    nc = tc.nc
    x_chunks = x.rearrange("(c p t) m k -> c p t (m k)", p=P, t=TILES)
    out_chunks = out.rearrange("(c p t) n -> c p t n", p=P, t=TILES)

    with ExitStack() as ctx:
        ctx.enter_context(tc.manual_schedule())
        keep = ctx.enter_context(tc.tile_pool(name="keep", bufs=1))
        xy_pool = ctx.enter_context(tc.tile_pool(name="xy_pool", bufs=CHUNKS + FRESH))
        mx_pool = ctx.enter_context(tc.tile_pool(name="mx_pool", bufs=4))
        xt_banks = ctx.enter_context(tc.psum_pool(name="xt_banks", bufs=4))
        acc_banks = ctx.enter_context(tc.psum_pool(name="acc_banks", bufs=4))

        x_tiles = {}
        grouped_tiles = {}
        code_tiles = {}
        plane_tiles = {}
        y_tiles = {}

        def load_tiles(first, count):
            c = first // TILES
            t = first % TILES
            if t == 0:
                x_tiles[c] = xy_pool.tile([P, TILES, MASKS * K], BF16, name="xy")
            nc.sync.dma_start(out=x_tiles[c][:, t : t + count, :], in_=x_chunks[c][:, t : t + count, :])

        def transpose_tile(i):
            grouped = mx_pool.tile([P, MASKS * K], BF16, name="grouped", align_bytes=64)
            grouped_tiles[i] = grouped
            x_words = x_tiles[i // TILES][:, i % TILES, :].bitcast(F32)
            grouped_words = grouped[:].bitcast(F32)
            for pair in range(PAIRS):
                xt = xt_banks.tile([P, 2, HALVES, P], F32, name="xt")
                for j in range(2):
                    first = (2 * pair + j) * (K // 2)
                    for u in range(HALVES):
                        nc.tensor.transpose(
                            xt[:, j, u, :],
                            x_words[:, first + u : first + K // 2 : HALVES],
                            ident[:],
                        )
                nc.scalar.copy(
                    out=grouped_words[:, pair * BANK : (pair + 1) * BANK].rearrange(
                        "p (j r u) -> p j r u", j=2, u=HALVES
                    ),
                    in_=xt[:].rearrange("p j u r -> p j r u"),
                )

        def quantise_tile(i):
            codes = mx_pool.tile([P, MASKS * P], U32, name="codes", align_bytes=64)
            planes = mx_pool.tile([P, MASKS * P], U8, name="planes", align_bytes=64)
            code_tiles[i] = codes
            plane_tiles[i] = planes
            nc.vector.quantize_mx(
                out=codes[:].bitcast(FP8X4), scales=planes[:], in_=grouped_tiles[i][:]
            )

        def multiply_tile(i):
            if i % TILES == 0:
                y_tiles[i // TILES] = xy_pool.tile([P, TILES, MASKS * U], F32, name="xy")
            y = y_tiles[i // TILES]
            for pair in range(PAIRS):
                acc = acc_banks.tile([P, BANK], F32, name="acc")
                for j in range(2):
                    m = 2 * pair + j
                    rows = slice(m * P, (m + 1) * P)
                    nc.tensor.matmul_mx(
                        out=acc[:, j * U : (j + 1) * U],
                        lhsT=code_tiles[i][:, rows].bitcast(FP8X4),
                        lhsT_scale=plane_tiles[i][:, rows],
                        rhs=w_codes[:, m, :].bitcast(FP8X4),
                        rhs_scale=w_planes[4 * m : P, :],
                        start=True,
                        stop=True,
                    )
                cols = slice(pair * BANK, (pair + 1) * BANK)
                nc.vector.tensor_tensor(
                    out=y[:, i % TILES, cols], in0=acc[:], in1=bias[:, cols], op=mybir.AluOpType.add
                )

        def relu_columns(i, first, count, scalar_share):
            y_row = y_tiles[i // TILES][:, i % TILES, :]
            split = first + scalar_share
            nc.scalar.activation(
                out=y_row[:, first:split],
                in_=y_row[:, first:split],
                func=mybir.ActivationFunctionType.Relu,
            )
            nc.gpsimd.tensor_scalar(
                out=y_row[:, split : first + count],
                in0=y_row[:, split : first + count],
                scalar1=float("inf"),
                scalar2=0.0,
                op0=mybir.AluOpType.min,
                op1=mybir.AluOpType.max,
            )

        def store_tiles(first, count):
            t = first % TILES
            nc.sync.dma_start(
                out=out_chunks[first // TILES][:, t : t + count, :],
                in_=y_tiles[first // TILES][:, t : t + count, :],
            )

        ident = keep.tile([P, P], F32, name="ident")
        make_identity(nc, ident[:])

        w_planes = keep.tile([P, U], U8, name="w_planes", align_bytes=64)
        nc.vector.memset(w_planes[:].bitcast(I32), 0)
        w_codes = keep.tile([P, MASKS, U], U32, name="w_codes", align_bytes=64)

        b_row = keep.tile([P, MASKS * U], BF16, name="b_row")
        nc.vector.memset(b_row[:], 0.0)
        ones = keep.tile([P, P], BF16, name="ones")
        nc.vector.memset(ones[:], 1.0)
        bias = keep.tile([P, MASKS * U], F32, name="bias")

        def load_scales_and_bias():
            scale_words = W_scales.bitcast(I32)
            for quadrant in range(4):
                nc.sync.dma_start(
                    out=w_planes[32 * quadrant : 32 * quadrant + 16, :].bitcast(I32),
                    in_=scale_words[:, 4 * quadrant : 4 * quadrant + 4, :],
                )
            nc.sync.dma_start(out=b_row[0:1, :], in_=b.rearrange("(o m) u -> o (m u)", o=1))

        loaded = 0
        for count in LOADS:
            if loaded == AHEAD - 1:
                load_scales_and_bias()
            if loaded == AHEAD:
                nc.sync.dma_start(
                    out=w_codes[:].bitcast(I32),
                    in_=W_words.rearrange("g p n t -> g p (n t)").bitcast(I32).rearrange("g p n -> p g n"),
                )
            load_tiles(loaded, count)
            loaded += count

        for i in range(AHEAD):
            transpose_tile(i)
        for i in range(AHEAD - 1):
            quantise_tile(i)
        for pair in range(PAIRS):
            cols = slice(pair * BANK, (pair + 1) * BANK)
            spread = acc_banks.tile([P, BANK], F32, name="acc")
            nc.tensor.matmul(out=spread[:], lhsT=ones[:], rhs=b_row[:, cols], start=True, stop=True)
            if pair == 0:
                nc.vector.tensor_copy(out=bias[:, cols], in_=spread[:])
            else:
                nc.scalar.copy(out=bias[:, cols], in_=spread[:])
        stores_done = 0
        stored = 0
        for i in range(ROW_TILES):
            multiply_tile(i)
            if i + AHEAD - 1 < ROW_TILES:
                quantise_tile(i + AHEAD - 1)
            if i >= 1:
                relu_columns(i - 1, 0, MASKS * U, SCALAR_RELU)
                if i == stored + STORES[stores_done]:
                    store_tiles(stored, STORES[stores_done])
                    stored = i
                    stores_done += 1
            if i + AHEAD < ROW_TILES:
                transpose_tile(i + AHEAD)

        last = ROW_TILES - 1
        for pair in range(PAIRS):
            cols = slice(pair * BANK, (pair + 1) * BANK)
            relu_columns(last, pair * BANK, BANK, SCALAR_RELU // PAIRS)
            nc.sync.dma_start(
                out=out_chunks[last // TILES][:, last % TILES, cols],
                in_=y_tiles[last // TILES][:, last % TILES, cols],
            )
